import numpy as np
import ml_dtypes

BF16 = ml_dtypes.bfloat16


def bf(x):
    return np.asarray(x, np.float32).astype(BF16)


def f32(x):
    return np.asarray(x, np.float32)


def f64(x):
    return np.asarray(x).astype(np.float64)


def striped(idx):
    return np.tile(idx.reshape(-1, 16).T, (8, 1))


C, C2, S, Q, K, N, O = 512, 1024, 2048, 1024, 4, 4096, 1024


def elu(v):
    return np.maximum(v, 0.0) + np.exp(np.minimum(v, 0.0)) - 1.0


def setup_inputs():
    idx = np.concatenate([np.random.permutation(S)[:Q] for _ in range(K)])
    return {"x": f32(np.random.standard_normal((C, S))), "w": bf(np.random.standard_normal((C2, O)) / np.sqrt(C2)), "b": f32(0.1 * np.random.standard_normal((O, 1))), "offs": striped(idx)}


def reference(x, w, b, offs):
    idx = offs[:16].T.reshape(-1)
    x, w, b = f64(x), f64(w), f64(b)
    xc = x[:, :Q]
    centre = w[:C].T @ xc + b
    res = None
    for k in range(K):
        d = x[:, idx[k * Q:(k + 1) * Q]] + (-xc)
        e = elu(centre + w[C:].T @ d)
        res = e if res is None else np.maximum(res, e)
    return res

@@ -1,0 +1,118 @@
+import concourse.mybir as mybir
+
+F32 = mybir.dt.float32
+BF16 = mybir.dt.bfloat16
+U16 = mybir.dt.uint16
+ADD = mybir.AluOpType.add
+MAX = mybir.AluOpType.max
+IDENTITY = mybir.ActivationFunctionType.Identity
+RELU = mybir.ActivationFunctionType.Relu
+EXP = mybir.ActivationFunctionType.Exp
+
+P = 128
+CHANNELS = 512
+NODES = 2048
+CENTRES = 1024
+NEIGHBOURS = 4
+FEATURES = 1024
+CB = CHANNELS // P
+FB = FEATURES // P
+BANK = 512
+HALVES = CENTRES // BANK
+AHEAD = 2
+
+FLOPS = 2 * FEATURES * CHANNELS * CENTRES * (1 + NEIGHBOURS)
+
+
+def tile_edgeconv_b_kernel(tc, x, w, b, offs, out):
+    nc = tc.nc
+    with (
+        tc.tile_pool(name="held", bufs=1) as held,
+        tc.tile_pool(name="sums", bufs=6) as sums,
+        tc.tile_pool(name="diffs", bufs=HALVES * NEIGHBOURS) as diffs,
+        tc.tile_pool(name="bests", bufs=2 * FB) as bests,
+        tc.tile_pool(name="work", bufs=3) as work,
+        tc.psum_pool(name="psum", bufs=8) as psum,
+    ):
+        offsets = held.tile([P, offs.shape[1]], U16, name="offsets")
+        nc.sync.dma_start(offsets[:], offs)
+        table = [held.tile([P, NODES], F32, name=f"table{c}") for c in range(CB)]
+        for lo, hi in ((0, BANK), (BANK, CENTRES), (CENTRES, NODES)):
+            for c in range(CB):
+                nc.sync.dma_start(table[c][:, lo:hi], x[c * P : (c + 1) * P, lo:hi])
+        weights = [held.tile([P, FEATURES], BF16, name=f"weights{r}") for r in range(2 * CB)]
+        bias = held.tile([P, FB], F32, name="bias")
+        for r in range(CB):
+            nc.scalar.dma_start(weights[r][:], w[r * P : (r + 1) * P, :])
+        with nc.allow_non_contiguous_dma(reason="one bias value to a partition, 4 KiB in all"):
+            nc.scalar.dma_start(bias[:], b.rearrange("(f p) o -> p (f o)", p=P))
+        for r in range(CB, 2 * CB):
+            nc.scalar.dma_start(weights[r][:], w[r * P : (r + 1) * P, :])
+
+        centre_bf = [held.tile([P, CENTRES], BF16, name=f"centre_bf{c}") for c in range(CB)]
+        minus_centre = [held.tile([P, CENTRES], F32, name=f"minus_centre{c}") for c in range(CB)]
+        for half in range(HALVES):
+            cols = slice(half * BANK, (half + 1) * BANK)
+            for c in range(CB):
+                nc.scalar.copy(centre_bf[c][:, cols], table[c][:, cols])
+        for c in range(CB):
+            nc.vector.tensor_scalar_mul(minus_centre[c][:], table[c][:, :CENTRES], -1.0)
+
+        def look_up_differences(half, k):
+            first = (k * CENTRES + half * BANK) // 16
+            piece = offsets[:, first : first + BANK // 16]
+            rounded = diffs.tile([P, CB, BANK], BF16, name="rounded")
+            for c in range(CB):
+                exact = sums.tile([P, BANK], F32, name="exact")
+                nc.vector.tensor_tensor(
+                    exact[:],
+                    table[c][:].indirect(piece),
+                    minus_centre[c][:, half * BANK : (half + 1) * BANK],
+                    ADD,
+                )
+                nc.scalar.copy(rounded[:, c, :], exact[:])
+            return rounded
+
+        def project(first_row_block, moving, f):
+            acc = psum.tile([P, BANK], F32, name="acc")
+            for c in range(CB):
+                nc.tensor.matmul(
+                    acc[:],
+                    weights[first_row_block + c][:, f * P : (f + 1) * P],
+                    moving[c],
+                    start=(c == 0),
+                    stop=(c == CB - 1),
+                )
+            return acc
+
+        pieces = [(half, k) for half in range(HALVES) for k in range(NEIGHBOURS)]
+        looked_up = [look_up_differences(half, k) for half, k in pieces[:AHEAD]]
+
+        centre_part = [held.tile([P, CENTRES], F32, name=f"centre_part{f}") for f in range(FB)]
+        for half in range(HALVES):
+            cols = slice(half * BANK, (half + 1) * BANK)
+            for f in range(FB):
+                acc = project(0, [centre_bf[c][:, cols] for c in range(CB)], f)
+                nc.scalar.activation(centre_part[f][:, cols], acc[:], IDENTITY, bias=bias[:, f : f + 1])
+
+        best = [None] * FB
+        for i, (half, k) in enumerate(pieces):
+            cols = slice(half * BANK, (half + 1) * BANK)
+            if i + AHEAD < len(pieces):
+                looked_up.append(look_up_differences(*pieces[i + AHEAD]))
+            for f in range(FB):
+                acc = project(CB, [looked_up[i][:, c, :] for c in range(CB)], f)
+                if k == 0:
+                    best[f] = bests.tile([P, BANK], F32, name="best")
+                    nc.scalar.copy(best[f][:], acc[:])
+                else:
+                    nc.vector.tensor_tensor(best[f][:], acc[:], best[f][:], MAX)
+                if k == NEIGHBOURS - 1:
+                    v = work.tile([P, BANK], F32, name="v")
+                    nc.gpsimd.tensor_tensor(v[:], best[f][:], centre_part[f][:, cols], ADD)
+                    e = work.tile([P, BANK], F32, name="e")
+                    nc.scalar.activation(e[:], v[:], RELU, scale=-1.0)
+                    nc.scalar.activation(e[:], e[:], EXP, scale=-1.0)
+                    result = work.tile([P, BANK], F32, name="result")
+                    nc.vector.scalar_tensor_tensor(result[:], e[:], -1.0, v[:], ADD, MAX)
+                    nc.sync.dma_start(out[f * P : (f + 1) * P, cols], result[:])

@@ -32,76 +32,86 @@ def tile_edgeconv_b_kernel(tc, x, w, b, offs, out):
         tc.tile_pool(name="diffs", bufs=HALVES * NEIGHBOURS) as diffs,
         tc.tile_pool(name="bests", bufs=2 * FB) as bests,
         tc.tile_pool(name="work", bufs=3) as work,
+        tc.tile_pool(name="results", bufs=HALVES * FB) as results,
         tc.psum_pool(name="psum", bufs=8) as psum,
     ):
         offsets = held.tile([P, offs.shape[1]], U16, name="offsets")
         nc.sync.dma_start(offsets[:], offs)
         table = [held.tile([P, NODES], F32, name=f"table{c}") for c in range(CB)]
+        weights = [held.tile([P, FEATURES], BF16, name=f"weights{r}") for r in range(2 * CB)]
+        bias = held.tile([P, FB], F32, name="bias")
+        with nc.allow_non_contiguous_dma(reason="one bias value to a partition, 4 KiB in all"):
+            nc.scalar.dma_start(bias[:], b.rearrange("(f p) o -> p (f o)", p=P))
+        for c in range(CB):
+            nc.scalar.dma_start(weights[c][:], w[c * P : (c + 1) * P, :])
         for lo, hi in ((0, BANK), (BANK, CENTRES), (CENTRES, NODES)):
             for c in range(CB):
                 nc.sync.dma_start(table[c][:, lo:hi], x[c * P : (c + 1) * P, lo:hi])
-        weights = [held.tile([P, FEATURES], BF16, name=f"weights{r}") for r in range(2 * CB)]
-        bias = held.tile([P, FB], F32, name="bias")
-        for r in range(CB):
-            nc.scalar.dma_start(weights[r][:], w[r * P : (r + 1) * P, :])
-        with nc.allow_non_contiguous_dma(reason="one bias value to a partition, 4 KiB in all"):
-            nc.scalar.dma_start(bias[:], b.rearrange("(f p) o -> p (f o)", p=P))
         for r in range(CB, 2 * CB):
-            nc.scalar.dma_start(weights[r][:], w[r * P : (r + 1) * P, :])
+            nc.sync.dma_start(weights[r][:], w[r * P : (r + 1) * P, :])
+
+        def columns(half):
+            return slice(half * BANK, (half + 1) * BANK)
 
         centre_bf = [held.tile([P, CENTRES], BF16, name=f"centre_bf{c}") for c in range(CB)]
         minus_centre = [held.tile([P, CENTRES], F32, name=f"minus_centre{c}") for c in range(CB)]
         for half in range(HALVES):
-            cols = slice(half * BANK, (half + 1) * BANK)
             for c in range(CB):
-                nc.scalar.copy(centre_bf[c][:, cols], table[c][:, cols])
-        for c in range(CB):
-            nc.vector.tensor_scalar_mul(minus_centre[c][:], table[c][:, :CENTRES], -1.0)
+                nc.vector.tensor_copy(centre_bf[c][:, columns(half)], table[c][:, columns(half)])
+                nc.vector.tensor_scalar_mul(minus_centre[c][:, columns(half)], table[c][:, columns(half)], -1.0)
 
         def look_up_differences(half, k):
             first = (k * CENTRES + half * BANK) // 16
-            piece = offsets[:, first : first + BANK // 16]
             rounded = diffs.tile([P, CB, BANK], BF16, name="rounded")
             for c in range(CB):
                 exact = sums.tile([P, BANK], F32, name="exact")
                 nc.vector.tensor_tensor(
                     exact[:],
-                    table[c][:].indirect(piece),
-                    minus_centre[c][:, half * BANK : (half + 1) * BANK],
+                    table[c][:].indirect(offsets[:, first : first + BANK // 16]),
+                    minus_centre[c][:, columns(half)],
                     ADD,
                 )
                 nc.scalar.copy(rounded[:, c, :], exact[:])
             return rounded
 
-        def project(first_row_block, moving, f):
-            acc = psum.tile([P, BANK], F32, name="acc")
-            for c in range(CB):
-                nc.tensor.matmul(
-                    acc[:],
-                    weights[first_row_block + c][:, f * P : (f + 1) * P],
-                    moving[c],
-                    start=(c == 0),
-                    stop=(c == CB - 1),
-                )
-            return acc
+        def multiply(acc, row_block, f, c, moving):
+            nc.tensor.matmul(
+                acc[:],
+                weights[row_block + c][:, f * P : (f + 1) * P],
+                moving,
+                start=(c == 0),
+                stop=(c == CB - 1),
+            )
 
         pieces = [(half, k) for half in range(HALVES) for k in range(NEIGHBOURS)]
         looked_up = [look_up_differences(half, k) for half, k in pieces[:AHEAD]]
 
         centre_part = [held.tile([P, CENTRES], F32, name=f"centre_part{f}") for f in range(FB)]
-        for half in range(HALVES):
-            cols = slice(half * BANK, (half + 1) * BANK)
-            for f in range(FB):
-                acc = project(0, [centre_bf[c][:, cols] for c in range(CB)], f)
-                nc.scalar.activation(centre_part[f][:, cols], acc[:], IDENTITY, bias=bias[:, f : f + 1])
+
+        def keep_centre_part(acc, half, f):
+            nc.scalar.activation(centre_part[f][:, columns(half)], acc[:], IDENTITY, bias=bias[:, f : f + 1])
+
+        groups = [(half, f) for half in range(HALVES) for f in range(FB)]
+        early = [(psum.tile([P, BANK], F32, name="acc"), half, f) for half, f in groups[:CB]]
+        for c in range(CB):
+            for acc, half, f in early:
+                multiply(acc, 0, f, c, centre_bf[c][:, columns(half)])
+        for acc, half, f in early:
+            keep_centre_part(acc, half, f)
+        for half, f in groups[CB:]:
+            acc = psum.tile([P, BANK], F32, name="acc")
+            for c in range(CB):
+                multiply(acc, 0, f, c, centre_bf[c][:, columns(half)])
+            keep_centre_part(acc, half, f)
 
         best = [None] * FB
         for i, (half, k) in enumerate(pieces):
-            cols = slice(half * BANK, (half + 1) * BANK)
             if i + AHEAD < len(pieces):
                 looked_up.append(look_up_differences(*pieces[i + AHEAD]))
             for f in range(FB):
-                acc = project(CB, [looked_up[i][:, c, :] for c in range(CB)], f)
+                acc = psum.tile([P, BANK], F32, name="acc")
+                for c in range(CB):
+                    multiply(acc, CB, f, c, looked_up[i][:, c, :])
                 if k == 0:
                     best[f] = bests.tile([P, BANK], F32, name="best")
                     nc.scalar.copy(best[f][:], acc[:])
@@ -109,10 +119,10 @@ def tile_edgeconv_b_kernel(tc, x, w, b, offs, out):
                     nc.vector.tensor_tensor(best[f][:], acc[:], best[f][:], MAX)
                 if k == NEIGHBOURS - 1:
                     v = work.tile([P, BANK], F32, name="v")
-                    nc.gpsimd.tensor_tensor(v[:], best[f][:], centre_part[f][:, cols], ADD)
+                    nc.gpsimd.tensor_tensor(v[:], best[f][:], centre_part[f][:, columns(half)], ADD)
                     e = work.tile([P, BANK], F32, name="e")
                     nc.scalar.activation(e[:], v[:], RELU, scale=-1.0)
                     nc.scalar.activation(e[:], e[:], EXP, scale=-1.0)
-                    result = work.tile([P, BANK], F32, name="result")
+                    result = results.tile([P, BANK], F32, name="result")
                     nc.vector.scalar_tensor_tensor(result[:], e[:], -1.0, v[:], ADD, MAX)
-                    nc.sync.dma_start(out[f * P : (f + 1) * P, cols], result[:])
+                    nc.sync.dma_start(out[f * P : (f + 1) * P, columns(half)], result[:])

@@ -119,7 +119,7 @@ def tile_edgeconv_b_kernel(tc, x, w, b, offs, out):
                     nc.vector.tensor_tensor(best[f][:], acc[:], best[f][:], MAX)
                 if k == NEIGHBOURS - 1:
                     v = work.tile([P, BANK], F32, name="v")
-                    nc.gpsimd.tensor_tensor(v[:], best[f][:], centre_part[f][:, columns(half)], ADD)
+                    nc.vector.tensor_tensor(v[:], best[f][:], centre_part[f][:, columns(half)], ADD)
                     e = work.tile([P, BANK], F32, name="e")
                     nc.scalar.activation(e[:], v[:], RELU, scale=-1.0)
                     nc.scalar.activation(e[:], e[:], EXP, scale=-1.0)

@@ -84,7 +84,13 @@ def tile_edgeconv_b_kernel(tc, x, w, b, offs, out):
             )
 
         pieces = [(half, k) for half in range(HALVES) for k in range(NEIGHBOURS)]
-        looked_up = [look_up_differences(half, k) for half, k in pieces[:AHEAD]]
+        looked_up = {}
+
+        def look_up_first(n):
+            for half, k in pieces[len(looked_up) : n]:
+                looked_up[(half, k)] = look_up_differences(half, k)
+
+        look_up_first(AHEAD)
 
         centre_part = [held.tile([P, CENTRES], F32, name=f"centre_part{f}") for f in range(FB)]
 
@@ -105,24 +111,25 @@ def tile_edgeconv_b_kernel(tc, x, w, b, offs, out):
             keep_centre_part(acc, half, f)
 
         best = [None] * FB
-        for i, (half, k) in enumerate(pieces):
-            if i + AHEAD < len(pieces):
-                looked_up.append(look_up_differences(*pieces[i + AHEAD]))
-            for f in range(FB):
-                acc = psum.tile([P, BANK], F32, name="acc")
-                for c in range(CB):
-                    multiply(acc, CB, f, c, looked_up[i][:, c, :])
-                if k == 0:
-                    best[f] = bests.tile([P, BANK], F32, name="best")
-                    nc.scalar.copy(best[f][:], acc[:])
-                else:
-                    nc.vector.tensor_tensor(best[f][:], acc[:], best[f][:], MAX)
-                if k == NEIGHBOURS - 1:
-                    v = work.tile([P, BANK], F32, name="v")
-                    nc.vector.tensor_tensor(v[:], best[f][:], centre_part[f][:, columns(half)], ADD)
-                    e = work.tile([P, BANK], F32, name="e")
-                    nc.scalar.activation(e[:], v[:], RELU, scale=-1.0)
-                    nc.scalar.activation(e[:], e[:], EXP, scale=-1.0)
-                    result = results.tile([P, BANK], F32, name="result")
-                    nc.vector.scalar_tensor_tensor(result[:], e[:], -1.0, v[:], ADD, MAX)
-                    nc.sync.dma_start(out[f * P : (f + 1) * P, columns(half)], result[:])
+        for half, stages in enumerate((((0,), (1,), (2,), (3,)), ((0,), (1, 2, 3)))):
+            for ks in stages:
+                look_up_first(half * NEIGHBOURS + ks[-1] + 1 + AHEAD)
+                for f in range(FB):
+                    for k in ks:
+                        acc = psum.tile([P, BANK], F32, name="acc")
+                        for c in range(CB):
+                            multiply(acc, CB, f, c, looked_up[(half, k)][:, c, :])
+                        if k == 0:
+                            best[f] = bests.tile([P, BANK], F32, name="best")
+                            nc.scalar.copy(best[f][:], acc[:])
+                        else:
+                            nc.vector.tensor_tensor(best[f][:], acc[:], best[f][:], MAX)
+                    if ks[-1] == NEIGHBOURS - 1:
+                        v = work.tile([P, BANK], F32, name="v")
+                        nc.vector.tensor_tensor(v[:], best[f][:], centre_part[f][:, columns(half)], ADD)
+                        e = work.tile([P, BANK], F32, name="e")
+                        nc.scalar.activation(e[:], v[:], RELU, scale=-1.0)
+                        nc.scalar.activation(e[:], e[:], EXP, scale=-1.0)
+                        result = results.tile([P, BANK], F32, name="result")
+                        nc.vector.scalar_tensor_tensor(result[:], e[:], -1.0, v[:], ADD, MAX)
+                        nc.sync.dma_start(out[f * P : (f + 1) * P, columns(half)], result[:])

@@ -28,41 +28,69 @@ def tile_edgeconv_b_kernel(tc, x, w, b, offs, out):
     nc = tc.nc
     with (
         tc.tile_pool(name="held", bufs=1) as held,
-        tc.tile_pool(name="sums", bufs=6) as sums,
-        tc.tile_pool(name="diffs", bufs=HALVES * NEIGHBOURS) as diffs,
-        tc.tile_pool(name="bests", bufs=2 * FB) as bests,
+        tc.tile_pool(name="moving", bufs=3) as moving,
+        tc.tile_pool(name="sums", bufs=3 * CB) as sums,
+        tc.tile_pool(name="seconds", bufs=FB) as seconds,
         tc.tile_pool(name="work", bufs=3) as work,
-        tc.tile_pool(name="results", bufs=HALVES * FB) as results,
+        tc.tile_pool(name="results", bufs=4) as results,
         tc.psum_pool(name="psum", bufs=8) as psum,
     ):
         offsets = held.tile([P, offs.shape[1]], U16, name="offsets")
-        nc.sync.dma_start(offsets[:], offs)
         table = [held.tile([P, NODES], F32, name=f"table{c}") for c in range(CB)]
         weights = [held.tile([P, FEATURES], BF16, name=f"weights{r}") for r in range(2 * CB)]
         bias = held.tile([P, FB], F32, name="bias")
-        with nc.allow_non_contiguous_dma(reason="one bias value to a partition, 4 KiB in all"):
-            nc.scalar.dma_start(bias[:], b.rearrange("(f p) o -> p (f o)", p=P))
         for c in range(CB):
             nc.scalar.dma_start(weights[c][:], w[c * P : (c + 1) * P, :])
+        with nc.allow_non_contiguous_dma(reason="one bias value to a partition, 4 KiB in all"):
+            nc.scalar.dma_start(bias[:], b.rearrange("(f p) o -> p (f o)", p=P))
         for lo, hi in ((0, BANK), (BANK, CENTRES), (CENTRES, NODES)):
             for c in range(CB):
                 nc.sync.dma_start(table[c][:, lo:hi], x[c * P : (c + 1) * P, lo:hi])
+            if lo == 0:
+                nc.sync.dma_start(offsets[:], offs)
         for r in range(CB, 2 * CB):
             nc.sync.dma_start(weights[r][:], w[r * P : (r + 1) * P, :])
 
         def columns(half):
             return slice(half * BANK, (half + 1) * BANK)
 
-        centre_bf = [held.tile([P, CENTRES], BF16, name=f"centre_bf{c}") for c in range(CB)]
+        centre_bf = moving.tile([P, CB, CENTRES], BF16, name="centre_bf", tag="moving")
         minus_centre = [held.tile([P, CENTRES], F32, name=f"minus_centre{c}") for c in range(CB)]
         for half in range(HALVES):
             for c in range(CB):
-                nc.vector.tensor_copy(centre_bf[c][:, columns(half)], table[c][:, columns(half)])
+                nc.vector.tensor_copy(centre_bf[:, c, columns(half)], table[c][:, columns(half)])
                 nc.vector.tensor_scalar_mul(minus_centre[c][:, columns(half)], table[c][:, columns(half)], -1.0)
+
+        def multiply(acc, row_block, f, c, operand):
+            nc.tensor.matmul(
+                acc[:],
+                weights[row_block + c][:, f * P : (f + 1) * P],
+                operand,
+                start=(c == 0),
+                stop=(c == CB - 1),
+            )
+
+        centre_part = [held.tile([P, CENTRES], F32, name=f"centre_part{f}") for f in range(FB)]
+
+        def keep_centre_part(acc, half, f):
+            nc.scalar.activation(centre_part[f][:, columns(half)], acc[:], IDENTITY, bias=bias[:, f : f + 1])
+
+        groups = [(half, f) for half in range(HALVES) for f in range(FB)]
+        early = [(psum.tile([P, BANK], F32, name="acc"), half, f) for half, f in groups[:CB]]
+        for c in range(CB):
+            for acc, half, f in early:
+                multiply(acc, 0, f, c, centre_bf[:, c, columns(half)])
+        for acc, half, f in early:
+            keep_centre_part(acc, half, f)
+        for half, f in groups[CB:]:
+            acc = psum.tile([P, BANK], F32, name="acc")
+            for c in range(CB):
+                multiply(acc, 0, f, c, centre_bf[:, c, columns(half)])
+            keep_centre_part(acc, half, f)
 
         def look_up_differences(half, k):
             first = (k * CENTRES + half * BANK) // 16
-            rounded = diffs.tile([P, CB, BANK], BF16, name="rounded")
+            rounded = moving.tile([P, CB, BANK], BF16, name="rounded", tag="moving")
             for c in range(CB):
                 exact = sums.tile([P, BANK], F32, name="exact")
                 nc.vector.tensor_tensor(
@@ -74,62 +102,49 @@ def tile_edgeconv_b_kernel(tc, x, w, b, offs, out):
                 nc.scalar.copy(rounded[:, c, :], exact[:])
             return rounded
 
-        def multiply(acc, row_block, f, c, moving):
-            nc.tensor.matmul(
-                acc[:],
-                weights[row_block + c][:, f * P : (f + 1) * P],
-                moving,
-                start=(c == 0),
-                stop=(c == CB - 1),
-            )
-
-        pieces = [(half, k) for half in range(HALVES) for k in range(NEIGHBOURS)]
+        pieces = [(half, k) for k_pair in ((0, 1), (2, 3)) for half in range(HALVES) for k in k_pair]
         looked_up = {}
 
         def look_up_first(n):
             for half, k in pieces[len(looked_up) : n]:
                 looked_up[(half, k)] = look_up_differences(half, k)
 
-        look_up_first(AHEAD)
-
-        centre_part = [held.tile([P, CENTRES], F32, name=f"centre_part{f}") for f in range(FB)]
-
-        def keep_centre_part(acc, half, f):
-            nc.scalar.activation(centre_part[f][:, columns(half)], acc[:], IDENTITY, bias=bias[:, f : f + 1])
-
-        groups = [(half, f) for half in range(HALVES) for f in range(FB)]
-        early = [(psum.tile([P, BANK], F32, name="acc"), half, f) for half, f in groups[:CB]]
-        for c in range(CB):
-            for acc, half, f in early:
-                multiply(acc, 0, f, c, centre_bf[c][:, columns(half)])
-        for acc, half, f in early:
-            keep_centre_part(acc, half, f)
-        for half, f in groups[CB:]:
-            acc = psum.tile([P, BANK], F32, name="acc")
+        def product(half, k, f, part=slice(0, BANK)):
+            acc = psum.tile([P, part.stop - part.start], F32, name="acc")
             for c in range(CB):
-                multiply(acc, 0, f, c, centre_bf[c][:, columns(half)])
-            keep_centre_part(acc, half, f)
+                multiply(acc, CB, f, c, looked_up[(half, k)][:, c, part])
+            return acc
 
-        best = [None] * FB
-        for half, stages in enumerate((((0,), (1,), (2,), (3,)), ((0,), (1, 2, 3)))):
-            for ks in stages:
-                look_up_first(half * NEIGHBOURS + ks[-1] + 1 + AHEAD)
-                for f in range(FB):
-                    for k in ks:
-                        acc = psum.tile([P, BANK], F32, name="acc")
-                        for c in range(CB):
-                            multiply(acc, CB, f, c, looked_up[(half, k)][:, c, :])
-                        if k == 0:
-                            best[f] = bests.tile([P, BANK], F32, name="best")
-                            nc.scalar.copy(best[f][:], acc[:])
-                        else:
-                            nc.vector.tensor_tensor(best[f][:], acc[:], best[f][:], MAX)
-                    if ks[-1] == NEIGHBOURS - 1:
-                        v = work.tile([P, BANK], F32, name="v")
-                        nc.vector.tensor_tensor(v[:], best[f][:], centre_part[f][:, columns(half)], ADD)
-                        e = work.tile([P, BANK], F32, name="e")
-                        nc.scalar.activation(e[:], v[:], RELU, scale=-1.0)
-                        nc.scalar.activation(e[:], e[:], EXP, scale=-1.0)
-                        result = results.tile([P, BANK], F32, name="result")
-                        nc.vector.scalar_tensor_tensor(result[:], e[:], -1.0, v[:], ADD, MAX)
-                        nc.sync.dma_start(out[f * P : (f + 1) * P, columns(half)], result[:])
+        best = {(half, f): held.tile([P, BANK], F32, name=f"best{half}{f}") for half in range(HALVES) for f in range(FB)}
+
+        for i, (half, k) in enumerate(pieces[: 2 * HALVES]):
+            look_up_first(i + 1 + AHEAD)
+            for f in range(FB):
+                acc = product(half, k, f)
+                if k == 0:
+                    nc.scalar.copy(best[(half, f)][:], acc[:])
+                else:
+                    second = seconds.tile([P, BANK], F32, name="second")
+                    nc.scalar.copy(second[:], acc[:])
+                    nc.vector.tensor_tensor(best[(half, f)][:], second[:], best[(half, f)][:], MAX)
+
+        whole_block = (slice(0, BANK),)
+        two_halves = (slice(0, BANK // 2), slice(BANK // 2, BANK))
+        for half in range(HALVES):
+            look_up_first(2 * HALVES + 2 * (half + 1) + AHEAD)
+            for f in range(FB):
+                last_block = half == HALVES - 1 and f == FB - 1
+                for part in two_halves if last_block else whole_block:
+                    width = part.stop - part.start
+                    centres = slice(half * BANK + part.start, half * BANK + part.stop)
+                    for k in (2, 3):
+                        acc = product(half, k, f, part)
+                        nc.vector.tensor_tensor(best[(half, f)][:, part], acc[:], best[(half, f)][:, part], MAX)
+                    v = work.tile([P, width], F32, name="v")
+                    nc.vector.tensor_tensor(v[:], best[(half, f)][:, part], centre_part[f][:, centres], ADD)
+                    e = work.tile([P, width], F32, name="e")
+                    nc.scalar.activation(e[:], v[:], RELU, scale=-1.0)
+                    nc.scalar.activation(e[:], e[:], EXP, scale=-1.0)
+                    result = results.tile([P, width], F32, name="result")
+                    nc.vector.scalar_tensor_tensor(result[:], e[:], -1.0, v[:], ADD, MAX)
+                    nc.sync.dma_start(out[f * P : (f + 1) * P, centres], result[:])

@@ -19,6 +19,7 @@ CB = CHANNELS // P
 FB = FEATURES // P
 BANK = 512
 HALVES = CENTRES // BANK
+LATE = 1
 AHEAD = 2
 
 FLOPS = 2 * FEATURES * CHANNELS * CENTRES * (1 + NEIGHBOURS)
@@ -43,10 +44,10 @@ def tile_edgeconv_b_kernel(tc, x, w, b, offs, out):
             nc.scalar.dma_start(weights[c][:], w[c * P : (c + 1) * P, :])
         with nc.allow_non_contiguous_dma(reason="one bias value to a partition, 4 KiB in all"):
             nc.scalar.dma_start(bias[:], b.rearrange("(f p) o -> p (f o)", p=P))
-        for lo, hi in ((0, BANK), (BANK, CENTRES), (CENTRES, NODES)):
+        for lo, hi in ((BANK, CENTRES), (0, BANK), (CENTRES, NODES)):
             for c in range(CB):
                 nc.sync.dma_start(table[c][:, lo:hi], x[c * P : (c + 1) * P, lo:hi])
-            if lo == 0:
+            if lo == BANK:
                 nc.sync.dma_start(offsets[:], offs)
         for r in range(CB, 2 * CB):
             nc.sync.dma_start(weights[r][:], w[r * P : (r + 1) * P, :])
@@ -54,11 +55,14 @@ def tile_edgeconv_b_kernel(tc, x, w, b, offs, out):
         def columns(half):
             return slice(half * BANK, (half + 1) * BANK)
 
-        centre_bf = moving.tile([P, CB, CENTRES], BF16, name="centre_bf", tag="moving")
+        centre_bf = [
+            moving.tile([P, CB, BANK], BF16, name="centre_bf0", tag="moving"),
+            held.tile([P, CB, BANK], BF16, name="centre_bf1"),
+        ]
         minus_centre = [held.tile([P, CENTRES], F32, name=f"minus_centre{c}") for c in range(CB)]
-        for half in range(HALVES):
+        for half in (1, 0):
             for c in range(CB):
-                nc.vector.tensor_copy(centre_bf[:, c, columns(half)], table[c][:, columns(half)])
+                nc.vector.tensor_copy(centre_bf[half][:, c, :], table[c][:, columns(half)])
                 nc.vector.tensor_scalar_mul(minus_centre[c][:, columns(half)], table[c][:, columns(half)], -1.0)
 
         def multiply(acc, row_block, f, c, operand):
@@ -75,17 +79,17 @@ def tile_edgeconv_b_kernel(tc, x, w, b, offs, out):
         def keep_centre_part(acc, half, f):
             nc.scalar.activation(centre_part[f][:, columns(half)], acc[:], IDENTITY, bias=bias[:, f : f + 1])
 
-        groups = [(half, f) for half in range(HALVES) for f in range(FB)]
+        groups = [(1, f) for f in range(FB - LATE)] + [(0, f) for f in range(FB)]
         early = [(psum.tile([P, BANK], F32, name="acc"), half, f) for half, f in groups[:CB]]
         for c in range(CB):
             for acc, half, f in early:
-                multiply(acc, 0, f, c, centre_bf[:, c, columns(half)])
+                multiply(acc, 0, f, c, centre_bf[half][:, c, :])
         for acc, half, f in early:
             keep_centre_part(acc, half, f)
         for half, f in groups[CB:]:
             acc = psum.tile([P, BANK], F32, name="acc")
             for c in range(CB):
-                multiply(acc, 0, f, c, centre_bf[:, c, columns(half)])
+                multiply(acc, 0, f, c, centre_bf[half][:, c, :])
             keep_centre_part(acc, half, f)
 
         def look_up_differences(half, k):
@@ -130,18 +134,29 @@ def tile_edgeconv_b_kernel(tc, x, w, b, offs, out):
 
         whole_block = (slice(0, BANK),)
         two_halves = (slice(0, BANK // 2), slice(BANK // 2, BANK))
+        steps = [(2, 0)]
+        for f in range(1, FB):
+            steps += [(2, f), (3, f - 1)]
+        steps += [(3, FB - 1)]
         for half in range(HALVES):
             look_up_first(2 * HALVES + 2 * (half + 1) + AHEAD)
-            for f in range(FB):
+            for k, f in steps:
                 last_block = half == HALVES - 1 and f == FB - 1
                 for part in two_halves if last_block else whole_block:
+                    acc = product(half, k, f, part)
+                    nc.vector.tensor_tensor(best[(half, f)][:, part], acc[:], best[(half, f)][:, part], MAX)
+                    if k == 2:
+                        continue
                     width = part.stop - part.start
                     centres = slice(half * BANK + part.start, half * BANK + part.stop)
-                    for k in (2, 3):
-                        acc = product(half, k, f, part)
-                        nc.vector.tensor_tensor(best[(half, f)][:, part], acc[:], best[(half, f)][:, part], MAX)
                     v = work.tile([P, width], F32, name="v")
-                    nc.vector.tensor_tensor(v[:], best[(half, f)][:, part], centre_part[f][:, centres], ADD)
+                    if half == HALVES - 1 and f >= FB - LATE:
+                        acc = psum.tile([P, width], F32, name="acc")
+                        for c in range(CB):
+                            multiply(acc, 0, f, c, centre_bf[half][:, c, part])
+                        nc.vector.scalar_tensor_tensor(v[:], acc[:], bias[:, f : f + 1], best[(half, f)][:, part], ADD, ADD)
+                    else:
+                        nc.vector.tensor_tensor(v[:], best[(half, f)][:, part], centre_part[f][:, centres], ADD)
                     e = work.tile([P, width], F32, name="e")
                     nc.scalar.activation(e[:], v[:], RELU, scale=-1.0)
                     nc.scalar.activation(e[:], e[:], EXP, scale=-1.0)

@@ -80,13 +80,13 @@ def tile_edgeconv_b_kernel(tc, x, w, b, offs, out):
             nc.scalar.activation(centre_part[f][:, columns(half)], acc[:], IDENTITY, bias=bias[:, f : f + 1])
 
         groups = [(1, f) for f in range(FB - LATE)] + [(0, f) for f in range(FB)]
-        early = [(psum.tile([P, BANK], F32, name="acc"), half, f) for half, f in groups[:CB]]
+        early = [(psum.tile([P, BANK], F32, name="acc"), half, f) for half, f in groups[: FB - LATE]]
         for c in range(CB):
             for acc, half, f in early:
                 multiply(acc, 0, f, c, centre_bf[half][:, c, :])
         for acc, half, f in early:
             keep_centre_part(acc, half, f)
-        for half, f in groups[CB:]:
+        for half, f in groups[FB - LATE :]:
             acc = psum.tile([P, BANK], F32, name="acc")
             for c in range(CB):
                 multiply(acc, 0, f, c, centre_bf[half][:, c, :])

@@ -4,7 +4,9 @@ F32 = mybir.dt.float32
 BF16 = mybir.dt.bfloat16
 U16 = mybir.dt.uint16
 ADD = mybir.AluOpType.add
+SUBTRACT = mybir.AluOpType.subtract
 MAX = mybir.AluOpType.max
+MIN = mybir.AluOpType.min
 IDENTITY = mybir.ActivationFunctionType.Identity
 RELU = mybir.ActivationFunctionType.Relu
 EXP = mybir.ActivationFunctionType.Exp
@@ -158,8 +160,14 @@ def tile_edgeconv_b_kernel(tc, x, w, b, offs, out):
                     else:
                         nc.vector.tensor_tensor(v[:], best[(half, f)][:, part], centre_part[f][:, centres], ADD)
                     e = work.tile([P, width], F32, name="e")
-                    nc.scalar.activation(e[:], v[:], RELU, scale=-1.0)
-                    nc.scalar.activation(e[:], e[:], EXP, scale=-1.0)
+                    positive = work.tile([P, width], F32, name="positive")
                     result = results.tile([P, width], F32, name="result")
-                    nc.vector.scalar_tensor_tensor(result[:], e[:], -1.0, v[:], ADD, MAX)
+                    nc.scalar.activation(e[:], v[:], EXP)
+                    if half == HALVES - 1 and f >= FB - 2:
+                        nc.vector.tensor_scalar(positive[:], v[:], 0.0, -1.0, MAX, ADD)
+                        nc.vector.scalar_tensor_tensor(result[:], e[:], 1.0, positive[:], MIN, ADD)
+                    else:
+                        nc.scalar.activation(positive[:], v[:], RELU)
+                        nc.scalar.activation(e[:], e[:], RELU, scale=-1.0, bias=1.0)
+                        nc.gpsimd.tensor_tensor(result[:], positive[:], e[:], SUBTRACT)
                     nc.sync.dma_start(out[f * P : (f + 1) * P, centres], result[:])

@@ -115,10 +115,10 @@ def tile_edgeconv_b_kernel(tc, x, w, b, offs, out):
             for half, k in pieces[len(looked_up) : n]:
                 looked_up[(half, k)] = look_up_differences(half, k)
 
-        def product(half, k, f, part=slice(0, BANK)):
-            acc = psum.tile([P, part.stop - part.start], F32, name="acc")
+        def product(half, k, f):
+            acc = psum.tile([P, BANK], F32, name="acc")
             for c in range(CB):
-                multiply(acc, CB, f, c, looked_up[(half, k)][:, c, part])
+                multiply(acc, CB, f, c, looked_up[(half, k)][:, c, :])
             return acc
 
         best = {(half, f): held.tile([P, BANK], F32, name=f"best{half}{f}") for half in range(HALVES) for f in range(FB)}
@@ -134,40 +134,58 @@ def tile_edgeconv_b_kernel(tc, x, w, b, offs, out):
                     nc.scalar.copy(second[:], acc[:])
                     nc.vector.tensor_tensor(best[(half, f)][:], second[:], best[(half, f)][:], MAX)
 
-        whole_block = (slice(0, BANK),)
-        two_halves = (slice(0, BANK // 2), slice(BANK // 2, BANK))
-        steps = [(2, 0)]
+        def elu_by_scalar_and_gpsimd(v):
+            e = work.tile([P, BANK], F32, name="e")
+            positive = work.tile([P, BANK], F32, name="positive")
+            result = results.tile([P, BANK], F32, name="result")
+            nc.scalar.activation(e[:], v[:], EXP)
+            nc.scalar.activation(positive[:], v[:], RELU)
+            nc.scalar.activation(e[:], e[:], RELU, scale=-1.0, bias=1.0)
+            nc.gpsimd.tensor_tensor(result[:], positive[:], e[:], SUBTRACT)
+            return result
+
+        def elu_by_scalar_and_vector(v, width):
+            e = work.tile([P, width], F32, name="e")
+            positive = work.tile([P, width], F32, name="positive")
+            result = results.tile([P, width], F32, name="result")
+            nc.scalar.activation(e[:], v[:], EXP)
+            nc.vector.tensor_scalar(positive[:], v[:], 0.0, -1.0, MAX, ADD)
+            nc.vector.scalar_tensor_tensor(result[:], e[:], 1.0, positive[:], MIN, ADD)
+            return result
+
+        def finish(half, f):
+            v = work.tile([P, BANK], F32, name="v")
+            nc.vector.tensor_tensor(v[:], best[(half, f)][:], centre_part[f][:, columns(half)], ADD)
+            if half == HALVES - 1 and f >= FB - 2:
+                result = elu_by_scalar_and_vector(v, BANK)
+            else:
+                result = elu_by_scalar_and_gpsimd(v)
+            nc.sync.dma_start(out[f * P : (f + 1) * P, columns(half)], result[:])
+
+        def finish_with_late_centre(half, f):
+            width = BANK // 2
+            for first in (0, width):
+                part = slice(first, first + width)
+                acc = psum.tile([P, width], F32, name="acc")
+                for c in range(CB):
+                    multiply(acc, 0, f, c, centre_bf[half][:, c, part])
+                v = work.tile([P, width], F32, name="v")
+                nc.vector.scalar_tensor_tensor(v[:], acc[:], bias[:, f : f + 1], best[(half, f)][:, part], ADD, ADD)
+                result = elu_by_scalar_and_vector(v, width)
+                nc.sync.dma_start(out[f * P : (f + 1) * P, half * BANK + first : half * BANK + first + width], result[:])
+
+        lagging = [(2, 0)]
         for f in range(1, FB):
-            steps += [(2, f), (3, f - 1)]
-        steps += [(3, FB - 1)]
-        for half in range(HALVES):
+            lagging += [(2, f), (3, f - 1)]
+        lagging += [(3, FB - 1)]
+        last_two_in_turn = lagging[:-3] + [(3, FB - 2), (2, FB - 1), (3, FB - 1)]
+        for half, steps in enumerate((lagging, last_two_in_turn)):
             look_up_first(2 * HALVES + 2 * (half + 1) + AHEAD)
             for k, f in steps:
-                last_block = half == HALVES - 1 and f == FB - 1
-                for part in two_halves if last_block else whole_block:
-                    acc = product(half, k, f, part)
-                    nc.vector.tensor_tensor(best[(half, f)][:, part], acc[:], best[(half, f)][:, part], MAX)
-                    if k == 2:
-                        continue
-                    width = part.stop - part.start
-                    centres = slice(half * BANK + part.start, half * BANK + part.stop)
-                    v = work.tile([P, width], F32, name="v")
+                acc = product(half, k, f)
+                nc.vector.tensor_tensor(best[(half, f)][:], acc[:], best[(half, f)][:], MAX)
+                if k == 3:
                     if half == HALVES - 1 and f >= FB - LATE:
-                        acc = psum.tile([P, width], F32, name="acc")
-                        for c in range(CB):
-                            multiply(acc, 0, f, c, centre_bf[half][:, c, part])
-                        nc.vector.scalar_tensor_tensor(v[:], acc[:], bias[:, f : f + 1], best[(half, f)][:, part], ADD, ADD)
+                        finish_with_late_centre(half, f)
                     else:
-                        nc.vector.tensor_tensor(v[:], best[(half, f)][:, part], centre_part[f][:, centres], ADD)
-                    e = work.tile([P, width], F32, name="e")
-                    positive = work.tile([P, width], F32, name="positive")
-                    result = results.tile([P, width], F32, name="result")
-                    nc.scalar.activation(e[:], v[:], EXP)
-                    if half == HALVES - 1 and f >= FB - 2:
-                        nc.vector.tensor_scalar(positive[:], v[:], 0.0, -1.0, MAX, ADD)
-                        nc.vector.scalar_tensor_tensor(result[:], e[:], 1.0, positive[:], MIN, ADD)
-                    else:
-                        nc.scalar.activation(positive[:], v[:], RELU)
-                        nc.scalar.activation(e[:], e[:], RELU, scale=-1.0, bias=1.0)
-                        nc.gpsimd.tensor_tensor(result[:], positive[:], e[:], SUBTRACT)
-                    nc.sync.dma_start(out[f * P : (f + 1) * P, centres], result[:])
+                        finish(half, f)

@@ -21,7 +21,7 @@ CB = CHANNELS // P
 FB = FEATURES // P
 BANK = 512
 HALVES = CENTRES // BANK
-LATE = 1
+LATE = 4
 AHEAD = 2
 
 FLOPS = 2 * FEATURES * CHANNELS * CENTRES * (1 + NEIGHBOURS)
@@ -156,36 +156,37 @@ def tile_edgeconv_b_kernel(tc, x, w, b, offs, out):
         def finish(half, f):
             v = work.tile([P, BANK], F32, name="v")
             nc.vector.tensor_tensor(v[:], best[(half, f)][:], centre_part[f][:, columns(half)], ADD)
-            if half == HALVES - 1 and f >= FB - 2:
-                result = elu_by_scalar_and_vector(v, BANK)
-            else:
-                result = elu_by_scalar_and_gpsimd(v)
+            result = elu_by_scalar_and_gpsimd(v)
             nc.sync.dma_start(out[f * P : (f + 1) * P, columns(half)], result[:])
 
-        def finish_with_late_centre(half, f):
-            width = BANK // 2
-            for first in (0, width):
+        def finish_with_late_centre(half, f, width):
+            for first in range(0, BANK, width):
                 part = slice(first, first + width)
                 acc = psum.tile([P, width], F32, name="acc")
                 for c in range(CB):
                     multiply(acc, 0, f, c, centre_bf[half][:, c, part])
                 v = work.tile([P, width], F32, name="v")
                 nc.vector.scalar_tensor_tensor(v[:], acc[:], bias[:, f : f + 1], best[(half, f)][:, part], ADD, ADD)
-                result = elu_by_scalar_and_vector(v, width)
+                if f == FB - 1:
+                    result = elu_by_scalar_and_vector(v, width)
+                else:
+                    result = elu_by_scalar_and_gpsimd(v)
                 nc.sync.dma_start(out[f * P : (f + 1) * P, half * BANK + first : half * BANK + first + width], result[:])
 
-        lagging = [(2, 0)]
-        for f in range(1, FB):
-            lagging += [(2, f), (3, f - 1)]
-        lagging += [(3, FB - 1)]
-        last_two_in_turn = lagging[:-3] + [(3, FB - 2), (2, FB - 1), (3, FB - 1)]
-        for half, steps in enumerate((lagging, last_two_in_turn)):
+        def take_maximum(half, k, f):
+            acc = product(half, k, f)
+            nc.vector.tensor_tensor(best[(half, f)][:], acc[:], best[(half, f)][:], MAX)
+
+        for half in range(HALVES):
             look_up_first(2 * HALVES + 2 * (half + 1) + AHEAD)
-            for k, f in steps:
-                acc = product(half, k, f)
-                nc.vector.tensor_tensor(best[(half, f)][:], acc[:], best[(half, f)][:], MAX)
-                if k == 3:
-                    if half == HALVES - 1 and f >= FB - LATE:
-                        finish_with_late_centre(half, f)
-                    else:
-                        finish(half, f)
+            late = LATE if half == HALVES - 1 else 0
+            for f in range(FB - late + 1):
+                if f < FB - late:
+                    take_maximum(half, 2, f)
+                if f > 0:
+                    take_maximum(half, 3, f - 1)
+                    finish(half, f - 1)
+            for f in range(FB - late, FB):
+                take_maximum(half, 2, f)
+                take_maximum(half, 3, f)
+                finish_with_late_centre(half, f, BANK // 2 if f == FB - 1 else BANK)

@@ -21,7 +21,7 @@ CB = CHANNELS // P
 FB = FEATURES // P
 BANK = 512
 HALVES = CENTRES // BANK
-LATE = 4
+LATE = 2
 AHEAD = 2
 
 FLOPS = 2 * FEATURES * CHANNELS * CENTRES * (1 + NEIGHBOURS)
@@ -46,10 +46,10 @@ def tile_edgeconv_b_kernel(tc, x, w, b, offs, out):
             nc.scalar.dma_start(weights[c][:], w[c * P : (c + 1) * P, :])
         with nc.allow_non_contiguous_dma(reason="one bias value to a partition, 4 KiB in all"):
             nc.scalar.dma_start(bias[:], b.rearrange("(f p) o -> p (f o)", p=P))
-        for lo, hi in ((BANK, CENTRES), (0, BANK), (CENTRES, NODES)):
+        for lo, hi in ((0, BANK), (BANK, CENTRES), (CENTRES, NODES)):
             for c in range(CB):
                 nc.sync.dma_start(table[c][:, lo:hi], x[c * P : (c + 1) * P, lo:hi])
-            if lo == BANK:
+            if lo == 0:
                 nc.sync.dma_start(offsets[:], offs)
         for r in range(CB, 2 * CB):
             nc.sync.dma_start(weights[r][:], w[r * P : (r + 1) * P, :])
@@ -62,7 +62,7 @@ def tile_edgeconv_b_kernel(tc, x, w, b, offs, out):
             held.tile([P, CB, BANK], BF16, name="centre_bf1"),
         ]
         minus_centre = [held.tile([P, CENTRES], F32, name=f"minus_centre{c}") for c in range(CB)]
-        for half in (1, 0):
+        for half in range(HALVES):
             for c in range(CB):
                 nc.vector.tensor_copy(centre_bf[half][:, c, :], table[c][:, columns(half)])
                 nc.vector.tensor_scalar_mul(minus_centre[c][:, columns(half)], table[c][:, columns(half)], -1.0)
@@ -81,14 +81,14 @@ def tile_edgeconv_b_kernel(tc, x, w, b, offs, out):
         def keep_centre_part(acc, half, f):
             nc.scalar.activation(centre_part[f][:, columns(half)], acc[:], IDENTITY, bias=bias[:, f : f + 1])
 
-        groups = [(1, f) for f in range(FB - LATE)] + [(0, f) for f in range(FB)]
-        early = [(psum.tile([P, BANK], F32, name="acc"), half, f) for half, f in groups[: FB - LATE]]
+        groups = [(0, f) for f in range(FB)] + [(1, f) for f in range(FB - LATE)]
+        early = [(psum.tile([P, BANK], F32, name="acc"), half, f) for half, f in groups[: FB - 1]]
         for c in range(CB):
             for acc, half, f in early:
                 multiply(acc, 0, f, c, centre_bf[half][:, c, :])
         for acc, half, f in early:
             keep_centre_part(acc, half, f)
-        for half, f in groups[FB - LATE :]:
+        for half, f in groups[FB - 1 :]:
             acc = psum.tile([P, BANK], F32, name="acc")
             for c in range(CB):
                 multiply(acc, 0, f, c, centre_bf[half][:, c, :])

@@ -42,17 +42,29 @@ def tile_edgeconv_b_kernel(tc, x, w, b, offs, out):
         table = [held.tile([P, NODES], F32, name=f"table{c}") for c in range(CB)]
         weights = [held.tile([P, FEATURES], BF16, name=f"weights{r}") for r in range(2 * CB)]
         bias = held.tile([P, FB], F32, name="bias")
+
+        def load_nodes(c, lo, hi):
+            nc.sync.dma_start(table[c][:, lo:hi], x[c * P : (c + 1) * P, lo:hi])
+
+        def load_weights(r, lo, hi):
+            nc.sync.dma_start(weights[r][:, lo:hi], w[r * P : (r + 1) * P, lo:hi])
+
         for c in range(CB):
-            nc.scalar.dma_start(weights[c][:], w[c * P : (c + 1) * P, :])
+            load_nodes(c, 0, BANK)
+            if c == 0:
+                load_weights(c, 0, 2 * P)
+                load_weights(c, 2 * P, FEATURES)
+            else:
+                load_weights(c, 0, FEATURES)
         with nc.allow_non_contiguous_dma(reason="one bias value to a partition, 4 KiB in all"):
-            nc.scalar.dma_start(bias[:], b.rearrange("(f p) o -> p (f o)", p=P))
-        for lo, hi in ((0, BANK), (BANK, CENTRES), (CENTRES, NODES)):
-            for c in range(CB):
-                nc.sync.dma_start(table[c][:, lo:hi], x[c * P : (c + 1) * P, lo:hi])
-            if lo == 0:
-                nc.sync.dma_start(offsets[:], offs)
+            nc.sync.dma_start(bias[:], b.rearrange("(f p) o -> p (f o)", p=P))
+        for c in range(CB):
+            load_nodes(c, BANK, CENTRES)
+        nc.sync.dma_start(offsets[:], offs)
+        for c in range(CB):
+            load_nodes(c, CENTRES, NODES)
         for r in range(CB, 2 * CB):
-            nc.sync.dma_start(weights[r][:], w[r * P : (r + 1) * P, :])
+            load_weights(r, 0, FEATURES)
 
         def columns(half):
             return slice(half * BANK, (half + 1) * BANK)

@@ -182,7 +182,11 @@ def tile_edgeconv_b_kernel(tc, x, w, b, offs, out):
                 if f == FB - 1:
                     result = elu_by_scalar_and_vector(v, width)
                 else:
-                    result = elu_by_scalar_and_gpsimd(v)
+                    e = work.tile([P, width], F32, name="e")
+                    result = results.tile([P, width], F32, name="result")
+                    nc.scalar.activation(e[:], v[:], RELU, scale=-1.0)
+                    nc.scalar.activation(e[:], e[:], EXP, scale=-1.0)
+                    nc.vector.scalar_tensor_tensor(result[:], e[:], -1.0, v[:], ADD, MAX)
                 nc.sync.dma_start(out[f * P : (f + 1) * P, half * BANK + first : half * BANK + first + width], result[:])
 
         def take_maximum(half, k, f):

@@ -7,7 +7,6 @@ ADD = mybir.AluOpType.add
 SUBTRACT = mybir.AluOpType.subtract
 MAX = mybir.AluOpType.max
 MIN = mybir.AluOpType.min
-IDENTITY = mybir.ActivationFunctionType.Identity
 RELU = mybir.ActivationFunctionType.Relu
 EXP = mybir.ActivationFunctionType.Exp
 
@@ -56,8 +55,6 @@ def tile_edgeconv_b_kernel(tc, x, w, b, offs, out):
                 load_weights(c, 2 * P, FEATURES)
             else:
                 load_weights(c, 0, FEATURES)
-        with nc.allow_non_contiguous_dma(reason="one bias value to a partition, 4 KiB in all"):
-            nc.sync.dma_start(bias[:], b.rearrange("(f p) o -> p (f o)", p=P))
         for c in range(CB):
             load_nodes(c, BANK, CENTRES)
         nc.sync.dma_start(offsets[:], offs)
@@ -65,6 +62,8 @@ def tile_edgeconv_b_kernel(tc, x, w, b, offs, out):
             load_nodes(c, CENTRES, NODES)
         for r in range(CB, 2 * CB):
             load_weights(r, 0, FEATURES)
+        with nc.allow_non_contiguous_dma(reason="one bias value to a partition, 4 KiB in all"):
+            nc.sync.dma_start(bias[:], b.rearrange("(f p) o -> p (f o)", p=P))
 
         def columns(half):
             return slice(half * BANK, (half + 1) * BANK)
@@ -77,7 +76,10 @@ def tile_edgeconv_b_kernel(tc, x, w, b, offs, out):
         for half in range(HALVES):
             for c in range(CB):
                 nc.vector.tensor_copy(centre_bf[half][:, c, :], table[c][:, columns(half)])
-                nc.vector.tensor_scalar_mul(minus_centre[c][:, columns(half)], table[c][:, columns(half)], -1.0)
+                if half == 0 and c == 0:
+                    nc.scalar.mul(minus_centre[c][:, columns(half)], table[c][:, columns(half)], -1.0)
+                else:
+                    nc.vector.tensor_scalar_mul(minus_centre[c][:, columns(half)], table[c][:, columns(half)], -1.0)
 
         def multiply(acc, row_block, f, c, operand):
             nc.tensor.matmul(
@@ -91,7 +93,7 @@ def tile_edgeconv_b_kernel(tc, x, w, b, offs, out):
         centre_part = [held.tile([P, CENTRES], F32, name=f"centre_part{f}") for f in range(FB)]
 
         def keep_centre_part(acc, half, f):
-            nc.scalar.activation(centre_part[f][:, columns(half)], acc[:], IDENTITY, bias=bias[:, f : f + 1])
+            nc.scalar.copy(centre_part[f][:, columns(half)], acc[:])
 
         groups = [(0, f) for f in range(FB)] + [(1, f) for f in range(FB - LATE)]
         early = [(psum.tile([P, BANK], F32, name="acc"), half, f) for half, f in groups[: FB - 1]]
@@ -167,7 +169,9 @@ def tile_edgeconv_b_kernel(tc, x, w, b, offs, out):
 
         def finish(half, f):
             v = work.tile([P, BANK], F32, name="v")
-            nc.vector.tensor_tensor(v[:], best[(half, f)][:], centre_part[f][:, columns(half)], ADD)
+            nc.vector.scalar_tensor_tensor(
+                v[:], best[(half, f)][:], bias[:, f : f + 1], centre_part[f][:, columns(half)], ADD, ADD
+            )
             result = elu_by_scalar_and_gpsimd(v)
             nc.sync.dma_start(out[f * P : (f + 1) * P, columns(half)], result[:])
 

import concourse.mybir as mybir

F32 = mybir.dt.float32
BF16 = mybir.dt.bfloat16
U16 = mybir.dt.uint16
ADD = mybir.AluOpType.add
SUBTRACT = mybir.AluOpType.subtract
MAX = mybir.AluOpType.max
MIN = mybir.AluOpType.min
RELU = mybir.ActivationFunctionType.Relu
EXP = mybir.ActivationFunctionType.Exp

P = 128
CHANNELS = 512
NODES = 2048
CENTRES = 1024
NEIGHBOURS = 4
FEATURES = 1024
CB = CHANNELS // P
FB = FEATURES // P
BANK = 512
HALVES = CENTRES // BANK
LATE = 2
AHEAD = 2

FLOPS = 2 * FEATURES * CHANNELS * CENTRES * (1 + NEIGHBOURS)


def tile_edgeconv_b_kernel(tc, x, w, b, offs, out):
    nc = tc.nc
    with (
        tc.tile_pool(name="held", bufs=1) as held,
        tc.tile_pool(name="moving", bufs=3) as moving,
        tc.tile_pool(name="sums", bufs=3 * CB) as sums,
        tc.tile_pool(name="seconds", bufs=FB) as seconds,
        tc.tile_pool(name="work", bufs=3) as work,
        tc.tile_pool(name="results", bufs=4) as results,
        tc.psum_pool(name="psum", bufs=8) as psum,
    ):
        offsets = held.tile([P, offs.shape[1]], U16, name="offsets")
        table = [held.tile([P, NODES], F32, name=f"table{c}") for c in range(CB)]
        weights = [held.tile([P, FEATURES], BF16, name=f"weights{r}") for r in range(2 * CB)]
        bias = held.tile([P, FB], F32, name="bias")

        def load_nodes(c, lo, hi):
            nc.sync.dma_start(table[c][:, lo:hi], x[c * P : (c + 1) * P, lo:hi])

        def load_weights(r, lo, hi):
            nc.sync.dma_start(weights[r][:, lo:hi], w[r * P : (r + 1) * P, lo:hi])

        for c in range(CB):
            load_nodes(c, 0, BANK)
            if c == 0:
                load_weights(c, 0, 2 * P)
                load_weights(c, 2 * P, FEATURES)
            else:
                load_weights(c, 0, FEATURES)
        for c in range(CB):
            load_nodes(c, BANK, CENTRES)
        nc.sync.dma_start(offsets[:], offs)
        for c in range(CB):
            load_nodes(c, CENTRES, NODES)
        for r in range(CB, 2 * CB):
            load_weights(r, 0, FEATURES)
        with nc.allow_non_contiguous_dma(reason="one bias value to a partition, 4 KiB in all"):
            nc.sync.dma_start(bias[:], b.rearrange("(f p) o -> p (f o)", p=P))

        def columns(half):
            return slice(half * BANK, (half + 1) * BANK)

        centre_bf = [
            moving.tile([P, CB, BANK], BF16, name="centre_bf0", tag="moving"),
            held.tile([P, CB, BANK], BF16, name="centre_bf1"),
        ]
        minus_centre = [held.tile([P, CENTRES], F32, name=f"minus_centre{c}") for c in range(CB)]
        for half in range(HALVES):
            for c in range(CB):
                nc.vector.tensor_copy(centre_bf[half][:, c, :], table[c][:, columns(half)])
                if half == 0 and c == 0:
                    nc.scalar.mul(minus_centre[c][:, columns(half)], table[c][:, columns(half)], -1.0)
                else:
                    nc.vector.tensor_scalar_mul(minus_centre[c][:, columns(half)], table[c][:, columns(half)], -1.0)

        def multiply(acc, row_block, f, c, operand):
            nc.tensor.matmul(
                acc[:],
                weights[row_block + c][:, f * P : (f + 1) * P],
                operand,
                start=(c == 0),
                stop=(c == CB - 1),
            )

        centre_part = [held.tile([P, CENTRES], F32, name=f"centre_part{f}") for f in range(FB)]

        def keep_centre_part(acc, half, f):
            nc.scalar.copy(centre_part[f][:, columns(half)], acc[:])

        groups = [(0, f) for f in range(FB)] + [(1, f) for f in range(FB - LATE)]
        early = [(psum.tile([P, BANK], F32, name="acc"), half, f) for half, f in groups[: FB - 1]]
        for c in range(CB):
            for acc, half, f in early:
                multiply(acc, 0, f, c, centre_bf[half][:, c, :])
        for acc, half, f in early:
            keep_centre_part(acc, half, f)
        for half, f in groups[FB - 1 :]:
            acc = psum.tile([P, BANK], F32, name="acc")
            for c in range(CB):
                multiply(acc, 0, f, c, centre_bf[half][:, c, :])
            keep_centre_part(acc, half, f)

        def look_up_differences(half, k):
            first = (k * CENTRES + half * BANK) // 16
            rounded = moving.tile([P, CB, BANK], BF16, name="rounded", tag="moving")
            for c in range(CB):
                exact = sums.tile([P, BANK], F32, name="exact")
                nc.vector.tensor_tensor(
                    exact[:],
                    table[c][:].indirect(offsets[:, first : first + BANK // 16]),
                    minus_centre[c][:, columns(half)],
                    ADD,
                )
                nc.scalar.copy(rounded[:, c, :], exact[:])
            return rounded

        pieces = [(half, k) for k_pair in ((0, 1), (2, 3)) for half in range(HALVES) for k in k_pair]
        looked_up = {}

        def look_up_first(n):
            for half, k in pieces[len(looked_up) : n]:
                looked_up[(half, k)] = look_up_differences(half, k)

        def product(half, k, f):
            acc = psum.tile([P, BANK], F32, name="acc")
            for c in range(CB):
                multiply(acc, CB, f, c, looked_up[(half, k)][:, c, :])
            return acc

        best = {(half, f): held.tile([P, BANK], F32, name=f"best{half}{f}") for half in range(HALVES) for f in range(FB)}

        for i, (half, k) in enumerate(pieces[: 2 * HALVES]):
            look_up_first(i + 1 + AHEAD)
            for f in range(FB):
                acc = product(half, k, f)
                if k == 0:
                    nc.scalar.copy(best[(half, f)][:], acc[:])
                else:
                    second = seconds.tile([P, BANK], F32, name="second")
                    nc.scalar.copy(second[:], acc[:])
                    nc.vector.tensor_tensor(best[(half, f)][:], second[:], best[(half, f)][:], MAX)

        def elu_by_scalar_and_gpsimd(v):
            e = work.tile([P, BANK], F32, name="e")
            positive = work.tile([P, BANK], F32, name="positive")
            result = results.tile([P, BANK], F32, name="result")
            nc.scalar.activation(e[:], v[:], EXP)
            nc.scalar.activation(positive[:], v[:], RELU)
            nc.scalar.activation(e[:], e[:], RELU, scale=-1.0, bias=1.0)
            nc.gpsimd.tensor_tensor(result[:], positive[:], e[:], SUBTRACT)
            return result

        def elu_by_scalar_and_vector(v, width):
            e = work.tile([P, width], F32, name="e")
            positive = work.tile([P, width], F32, name="positive")
            result = results.tile([P, width], F32, name="result")
            nc.scalar.activation(e[:], v[:], EXP)
            nc.vector.tensor_scalar(positive[:], v[:], 0.0, -1.0, MAX, ADD)
            nc.vector.scalar_tensor_tensor(result[:], e[:], 1.0, positive[:], MIN, ADD)
            return result

        def finish(half, f):
            v = work.tile([P, BANK], F32, name="v")
            nc.vector.scalar_tensor_tensor(
                v[:], best[(half, f)][:], bias[:, f : f + 1], centre_part[f][:, columns(half)], ADD, ADD
            )
            result = elu_by_scalar_and_gpsimd(v)
            nc.sync.dma_start(out[f * P : (f + 1) * P, columns(half)], result[:])

        def finish_with_late_centre(half, f, width):
            for first in range(0, BANK, width):
                part = slice(first, first + width)
                acc = psum.tile([P, width], F32, name="acc")
                for c in range(CB):
                    multiply(acc, 0, f, c, centre_bf[half][:, c, part])
                v = work.tile([P, width], F32, name="v")
                nc.vector.scalar_tensor_tensor(v[:], acc[:], bias[:, f : f + 1], best[(half, f)][:, part], ADD, ADD)
                if f == FB - 1:
                    result = elu_by_scalar_and_vector(v, width)
                else:
                    e = work.tile([P, width], F32, name="e")
                    result = results.tile([P, width], F32, name="result")
                    nc.scalar.activation(e[:], v[:], RELU, scale=-1.0)
                    nc.scalar.activation(e[:], e[:], EXP, scale=-1.0)
                    nc.vector.scalar_tensor_tensor(result[:], e[:], -1.0, v[:], ADD, MAX)
                nc.sync.dma_start(out[f * P : (f + 1) * P, half * BANK + first : half * BANK + first + width], result[:])

        def take_maximum(half, k, f):
            acc = product(half, k, f)
            nc.vector.tensor_tensor(best[(half, f)][:], acc[:], best[(half, f)][:], MAX)

        for half in range(HALVES):
            look_up_first(2 * HALVES + 2 * (half + 1) + AHEAD)
            late = LATE if half == HALVES - 1 else 0
            for f in range(FB - late + 1):
                if f < FB - late:
                    take_maximum(half, 2, f)
                if f > 0:
                    take_maximum(half, 3, f - 1)
                    finish(half, f - 1)
            for f in range(FB - late, FB):
                take_maximum(half, 2, f)
                take_maximum(half, 3, f)
                finish_with_late_centre(half, f, BANK // 2 if f == FB - 1 else BANK)
